import numpy as np
import ml_dtypes


def mxq(x, axis, fmt="e4m3"):
    dtype, down = {"e4m3": (ml_dtypes.float8_e4m3fn, 7), "e5m2": (ml_dtypes.float8_e5m2, 14)}[fmt]
    v = np.moveaxis(np.asarray(x, np.float32).astype(ml_dtypes.bfloat16).astype(np.float64), axis, -1)
    blocks = v.reshape(v.shape[:-1] + (-1, 32))
    amax = np.abs(blocks).max(-1, keepdims=True)
    byte = np.maximum(np.where(amax > 0, np.frexp(amax)[1] - 1 + 127, 0) - down, 1)
    scale = np.exp2(byte - 127.0)
    codes = (blocks / scale).astype(np.float32).astype(dtype).astype(np.float64)
    return np.moveaxis((codes * scale).reshape(v.shape), -1, axis)


WIDE = False


def mx_kscale(k):
    if not WIDE:
        return np.ones(k)
    levels = np.array([20, -20, 10, -10, 0])
    a = np.random.permutation(np.resize(levels, k // 512 * 4)).reshape(k // 512, 4)
    idx = np.arange(k)
    return np.exp2(a[idx // 512, idx % 128 // 32])


BF16 = ml_dtypes.bfloat16


def bf(x):
    return np.asarray(x, np.float32).astype(BF16)


def f64(x):
    return np.asarray(x).astype(np.float64)


NM, B, IN, H1, H2, OUT = 8, 512, 512, 512, 512, 128
LS_LO, LS_HI = -20.0, 4.0


def fnoise(ei, ej):
    return np.sign(ei) * np.sign(ej) * np.sqrt(np.abs(ei)) * np.sqrt(np.abs(ej))


def plin0(x, w, b):
    y = x.transpose(1, 0, 2) @ w.transpose(0, 2, 1)
    return y.transpose(1, 0, 2) + b[None]


def preact(s, ei1, ej1, w11, b11, w12, b12):
    sf = f64(s)
    mu = plin0(sf, f64(w11), f64(b11))
    log_sigma = np.clip(plin0(sf, f64(w12), f64(b12)), LS_LO, LS_HI)
    return mu + fnoise(f64(ei1), f64(ej1)) * np.exp(log_sigma)


def setup_inputs():
    k = mx_kscale(B)[:, None, None]
    s0 = bf(np.random.standard_normal((B, NM, IN)))
    ei1 = bf(np.random.standard_normal((B, NM, 1)))
    ej1 = bf(np.random.standard_normal((1, NM, H1)))
    w11 = bf(np.random.standard_normal((NM, H1, IN)) / np.sqrt(IN))
    b11 = bf(np.random.standard_normal((NM, H1)) * 0.3)
    w12 = bf(np.random.standard_normal((NM, H1, IN)) * 1.2 / np.sqrt(IN))
    b12 = bf(np.random.standard_normal((NM, H1)) * 0.3)
    g = bf(np.random.standard_normal((B, NM, H1)) * np.exp2(np.random.randint(-12, 1, (B, NM, 1))) / k)
    h = preact(s0, ei1, ej1, w11, b11, w12, b12)
    return {'s': bf(f64(s0) * k), 'ei1': ei1, 'ej1': ej1, 'w11': w11, 'b11': b11, 'w12': w12, 'b12': b12,
            'h': np.asarray(h, np.float32), 'grad_out': g}


def reference(s, ei1, ej1, w11, b11, w12, b12, h, grad_out):
    dh = f64(grad_out) * (f64(h) > 0.0)
    dq = mxq(dh, 0, 'e5m2')
    sq = mxq(f64(s), 0, 'e4m3')
    return dq.transpose(1, 2, 0) @ sq.transpose(1, 0, 2)

@@ -1,0 +1,118 @@
+import concourse.mybir as mybir
+
+BF16 = mybir.dt.bfloat16
+F32 = mybir.dt.float32
+U32 = mybir.dt.uint32
+U8 = mybir.dt.uint8
+E4M3_X4 = mybir.dt.float8_e4m3fn_x4
+E5M2_X4 = mybir.dt.float8_e5m2_x4
+ALU = mybir.AluOpType
+
+P = 128
+PACK = 4
+ROWS = P * PACK
+MODULES = 8
+UNITS = 512
+FEATURES = 512
+UNIT_TILES = UNITS // P
+CHUNK = 2
+CHUNKS = MODULES // CHUNK
+
+FLOPS = 2 * MODULES * UNITS * FEATURES * ROWS
+BYTES = MODULES * ROWS * (2 * FEATURES + 2 * UNITS + 4 * UNITS) + 4 * MODULES * UNITS * FEATURES
+
+
+def tile_skill_net_pa_v_kernel(tc, s, ei1, ej1, w11, b11, w12, b12, h, grad_out, out):
+    nc = tc.nc
+
+    s_rows = s.rearrange("(p t) j f -> p t j f", t=PACK)
+    g_rows = grad_out.rearrange("(p t) j l -> p t j l", t=PACK)
+    h_rows = h.rearrange("(p t) j l -> p t j l", t=PACK)
+    out_rows = out.rearrange("j (m b) f -> j m b f", b=UNIT_TILES)
+
+    with (
+        tc.tile_pool(name="loads", bufs=CHUNKS) as loads,
+        tc.tile_pool(name="grouped", bufs=2) as grouped,
+        tc.tile_pool(name="quantised", bufs=2) as quantised,
+        tc.tile_pool(name="results", bufs=MODULES) as results,
+        tc.psum_pool(name="psum", bufs=8) as psum,
+    ):
+        s_chunks, g_chunks, h_chunks = [], [], []
+        for c in range(CHUNKS):
+            modules = slice(c * CHUNK, (c + 1) * CHUNK)
+            s_in = loads.tile([P, PACK, CHUNK, FEATURES], BF16)
+            nc.sync.dma_start(out=s_in[:], in_=s_rows[:, :, modules, :])
+            g_in = loads.tile([P, PACK, CHUNK, UNITS], BF16)
+            nc.sync.dma_start(out=g_in[:], in_=g_rows[:, :, modules, :])
+            h_in = loads.tile([P, PACK, CHUNK, UNITS], F32)
+            nc.sync.dma_start(out=h_in[:], in_=h_rows[:, :, modules, :])
+            s_chunks.append(s_in)
+            g_chunks.append(g_in)
+            h_chunks.append(h_in)
+
+        def quantise_s(j):
+            s_module = s_chunks[j // CHUNK][:, :, j % CHUNK, :]
+            s_grouped = grouped.tile([P, FEATURES, PACK], BF16, align_bytes=64)
+            nc.scalar.copy(
+                out=s_grouped[:].rearrange("p (c i) t -> p c t i", i=4),
+                in_=s_module.rearrange("p t (c i) -> p c t i", i=4),
+            )
+            s_codes = quantised.tile([P, FEATURES], U32, align_bytes=64)
+            s_scales = quantised.tile([P, FEATURES], U8, align_bytes=64)
+            nc.vector.quantize_mx(
+                out=s_codes[:].bitcast(E4M3_X4),
+                scales=s_scales[:],
+                in_=s_grouped[:].rearrange("p f t -> p (f t)"),
+            )
+            return s_codes, s_scales
+
+        def mask_dh(j):
+            g_module = g_chunks[j // CHUNK][:, :, j % CHUNK, :]
+            h_module = h_chunks[j // CHUNK][:, :, j % CHUNK, :]
+            dh_grouped = grouped.tile([P, UNIT_TILES, P, PACK], BF16, align_bytes=64)
+            for b in range(UNIT_TILES):
+                nc.vector.scalar_tensor_tensor(
+                    out=dh_grouped[:, b, :, :],
+                    in0=h_module.rearrange("p t (m b) -> p b m t", b=UNIT_TILES)[:, b, :, :],
+                    scalar=0.0,
+                    in1=g_module.rearrange("p t (m b) -> p b m t", b=UNIT_TILES)[:, b, :, :],
+                    op0=ALU.is_gt,
+                    op1=ALU.mult,
+                )
+            return dh_grouped
+
+        def quantise_dh(dh_grouped):
+            dh_codes = quantised.tile([P, UNITS], U32, align_bytes=64)
+            dh_scales = quantised.tile([P, UNITS], U8, align_bytes=64)
+            nc.vector.quantize_mx(
+                out=dh_codes[:].bitcast(E5M2_X4),
+                scales=dh_scales[:],
+                in_=dh_grouped[:].rearrange("p b m t -> p (b m t)"),
+            )
+            return dh_codes, dh_scales
+
+        def multiply_and_store(j, dh_codes, dh_scales, s_codes, s_scales):
+            result = results.tile([P, UNIT_TILES, FEATURES], F32)
+            for b in range(UNIT_TILES):
+                units = slice(b * P, (b + 1) * P)
+                acc = psum.tile([P, FEATURES], F32)
+                nc.tensor.matmul_mx(
+                    out=acc[:],
+                    lhsT=dh_codes[:, units].bitcast(E5M2_X4),
+                    lhsT_scale=dh_scales[:, units],
+                    rhs=s_codes[:].bitcast(E4M3_X4),
+                    rhs_scale=s_scales[:],
+                    start=True,
+                    stop=True,
+                )
+                nc.scalar.copy(out=result[:, b, :], in_=acc[:])
+            nc.sync.dma_start(out=out_rows[j], in_=result[:])
+
+        operands = {}
+        for j in range(MODULES + 1):
+            if j < MODULES:
+                dh_grouped = mask_dh(j)
+                s_operand = quantise_s(j)
+                operands[j] = quantise_dh(dh_grouped) + s_operand
+            if j > 0:
+                multiply_and_store(j - 1, *operands[j - 1])

@@ -50,13 +50,16 @@ def tile_skill_net_pa_v_kernel(tc, s, ei1, ej1, w11, b11, w12, b12, h, grad_out,
             g_chunks.append(g_in)
             h_chunks.append(h_in)
 
-        def quantise_s(j):
+        def regroup_s(j):
             s_module = s_chunks[j // CHUNK][:, :, j % CHUNK, :]
             s_grouped = grouped.tile([P, FEATURES, PACK], BF16, align_bytes=64)
             nc.scalar.copy(
                 out=s_grouped[:].rearrange("p (c i) t -> p c t i", i=4),
                 in_=s_module.rearrange("p t (c i) -> p c t i", i=4),
             )
+            return s_grouped
+
+        def quantise_s(s_grouped):
             s_codes = quantised.tile([P, FEATURES], U32, align_bytes=64)
             s_scales = quantised.tile([P, FEATURES], U8, align_bytes=64)
             nc.vector.quantize_mx(
@@ -69,16 +72,17 @@ def tile_skill_net_pa_v_kernel(tc, s, ei1, ej1, w11, b11, w12, b12, h, grad_out,
         def mask_dh(j):
             g_module = g_chunks[j // CHUNK][:, :, j % CHUNK, :]
             h_module = h_chunks[j // CHUNK][:, :, j % CHUNK, :]
+            nc.vector.scalar_tensor_tensor(
+                out=g_module, in0=h_module, scalar=0.0, in1=g_module, op0=ALU.is_gt, op1=ALU.mult
+            )
+            return g_module
+
+        def regroup_dh(dh_module):
             dh_grouped = grouped.tile([P, UNIT_TILES, P, PACK], BF16, align_bytes=64)
-            for b in range(UNIT_TILES):
-                nc.vector.scalar_tensor_tensor(
-                    out=dh_grouped[:, b, :, :],
-                    in0=h_module.rearrange("p t (m b) -> p b m t", b=UNIT_TILES)[:, b, :, :],
-                    scalar=0.0,
-                    in1=g_module.rearrange("p t (m b) -> p b m t", b=UNIT_TILES)[:, b, :, :],
-                    op0=ALU.is_gt,
-                    op1=ALU.mult,
-                )
+            nc.vector.tensor_copy(
+                out=dh_grouped[:].rearrange("p b m t -> p m t b"),
+                in_=dh_module.rearrange("p t (m b) -> p m t b", b=UNIT_TILES),
+            )
             return dh_grouped
 
         def quantise_dh(dh_grouped):
@@ -108,11 +112,13 @@ def tile_skill_net_pa_v_kernel(tc, s, ei1, ej1, w11, b11, w12, b12, h, grad_out,
                 nc.scalar.copy(out=result[:, b, :], in_=acc[:])
             nc.sync.dma_start(out=out_rows[j], in_=result[:])
 
-        operands = {}
+        dh_ready, s_ready = {}, {}
         for j in range(MODULES + 1):
             if j < MODULES:
-                dh_grouped = mask_dh(j)
-                s_operand = quantise_s(j)
-                operands[j] = quantise_dh(dh_grouped) + s_operand
+                s_grouped = regroup_s(j)
+                dh_module = mask_dh(j)
             if j > 0:
-                multiply_and_store(j - 1, *operands[j - 1])
+                multiply_and_store(j - 1, *quantise_dh(dh_ready[j - 1]), *s_ready[j - 1])
+            if j < MODULES:
+                dh_ready[j] = regroup_dh(dh_module)
+                s_ready[j] = quantise_s(s_grouped)

@@ -15,8 +15,8 @@ MODULES = 8
 UNITS = 512
 FEATURES = 512
 UNIT_TILES = UNITS // P
-CHUNK = 2
-CHUNKS = MODULES // CHUNK
+CHUNK_SIZES = (1, 1, 2, 2, 2)
+assert sum(CHUNK_SIZES) == MODULES
 
 FLOPS = 2 * MODULES * UNITS * FEATURES * ROWS
 BYTES = MODULES * ROWS * (2 * FEATURES + 2 * UNITS + 4 * UNITS) + 4 * MODULES * UNITS * FEATURES
@@ -31,31 +31,33 @@ def tile_skill_net_pa_v_kernel(tc, s, ei1, ej1, w11, b11, w12, b12, h, grad_out,
     out_rows = out.rearrange("j (m b) f -> j m b f", b=UNIT_TILES)
 
     with (
-        tc.tile_pool(name="loads", bufs=CHUNKS) as loads,
-        tc.tile_pool(name="grouped", bufs=2) as grouped,
+        tc.tile_pool(name="loads", bufs=1) as loads,
+        tc.tile_pool(name="grouped", bufs=3) as grouped,
         tc.tile_pool(name="quantised", bufs=2) as quantised,
         tc.tile_pool(name="results", bufs=MODULES) as results,
         tc.psum_pool(name="psum", bufs=8) as psum,
+        tc.manual_schedule(),
     ):
-        s_chunks, g_chunks, h_chunks = [], [], []
-        for c in range(CHUNKS):
-            modules = slice(c * CHUNK, (c + 1) * CHUNK)
-            s_in = loads.tile([P, PACK, CHUNK, FEATURES], BF16)
-            nc.sync.dma_start(out=s_in[:], in_=s_rows[:, :, modules, :])
-            g_in = loads.tile([P, PACK, CHUNK, UNITS], BF16)
+        s_modules, g_modules, h_modules = [], [], []
+        first = 0
+        for size in CHUNK_SIZES:
+            modules = slice(first, first + size)
+            g_in = loads.tile([P, PACK, size, UNITS], BF16, name="g_in%d" % first)
             nc.sync.dma_start(out=g_in[:], in_=g_rows[:, :, modules, :])
-            h_in = loads.tile([P, PACK, CHUNK, UNITS], F32)
+            h_in = loads.tile([P, PACK, size, UNITS], F32, name="h_in%d" % first)
             nc.sync.dma_start(out=h_in[:], in_=h_rows[:, :, modules, :])
-            s_chunks.append(s_in)
-            g_chunks.append(g_in)
-            h_chunks.append(h_in)
+            s_in = loads.tile([P, PACK, size, FEATURES], BF16, name="s_in%d" % first)
+            nc.sync.dma_start(out=s_in[:], in_=s_rows[:, :, modules, :])
+            g_modules.extend([g_in[:, :, n, :] for n in range(size)])
+            h_modules.extend([h_in[:, :, n, :] for n in range(size)])
+            s_modules.extend([s_in[:, :, n, :] for n in range(size)])
+            first += size
 
         def regroup_s(j):
-            s_module = s_chunks[j // CHUNK][:, :, j % CHUNK, :]
             s_grouped = grouped.tile([P, FEATURES, PACK], BF16, align_bytes=64)
             nc.scalar.copy(
                 out=s_grouped[:].rearrange("p (c i) t -> p c t i", i=4),
-                in_=s_module.rearrange("p t (c i) -> p c t i", i=4),
+                in_=s_modules[j].rearrange("p t (c i) -> p c t i", i=4),
             )
             return s_grouped
 
@@ -70,12 +72,15 @@ def tile_skill_net_pa_v_kernel(tc, s, ei1, ej1, w11, b11, w12, b12, h, grad_out,
             return s_codes, s_scales
 
         def mask_dh(j):
-            g_module = g_chunks[j // CHUNK][:, :, j % CHUNK, :]
-            h_module = h_chunks[j // CHUNK][:, :, j % CHUNK, :]
             nc.vector.scalar_tensor_tensor(
-                out=g_module, in0=h_module, scalar=0.0, in1=g_module, op0=ALU.is_gt, op1=ALU.mult
+                out=g_modules[j],
+                in0=h_modules[j],
+                scalar=0.0,
+                in1=g_modules[j],
+                op0=ALU.is_gt,
+                op1=ALU.mult,
             )
-            return g_module
+            return g_modules[j]
 
         def regroup_dh(dh_module):
             dh_grouped = grouped.tile([P, UNIT_TILES, P, PACK], BF16, align_bytes=64)
@@ -95,8 +100,8 @@ def tile_skill_net_pa_v_kernel(tc, s, ei1, ej1, w11, b11, w12, b12, h, grad_out,
             )
             return dh_codes, dh_scales
 
-        def multiply_and_store(j, dh_codes, dh_scales, s_codes, s_scales):
-            result = results.tile([P, UNIT_TILES, FEATURES], F32)
+        def multiply(dh_codes, dh_scales, s_codes, s_scales):
+            banks = []
             for b in range(UNIT_TILES):
                 units = slice(b * P, (b + 1) * P)
                 acc = psum.tile([P, FEATURES], F32)
@@ -109,16 +114,25 @@ def tile_skill_net_pa_v_kernel(tc, s, ei1, ej1, w11, b11, w12, b12, h, grad_out,
                     start=True,
                     stop=True,
                 )
-                nc.scalar.copy(out=result[:, b, :], in_=acc[:])
+                banks.append(acc)
+            return banks
+
+        def store(j, banks):
+            result = results.tile([P, UNIT_TILES, FEATURES], F32)
+            for b in range(UNIT_TILES):
+                nc.scalar.copy(out=result[:, b, :], in_=banks[b][:])
             nc.sync.dma_start(out=out_rows[j], in_=result[:])
 
-        dh_ready, s_ready = {}, {}
-        for j in range(MODULES + 1):
+        regrouped_s, regrouped_dh, products = {}, {}, {}
+        for j in range(MODULES + 2):
             if j < MODULES:
-                s_grouped = regroup_s(j)
+                regrouped_s[j] = regroup_s(j)
                 dh_module = mask_dh(j)
-            if j > 0:
-                multiply_and_store(j - 1, *quantise_dh(dh_ready[j - 1]), *s_ready[j - 1])
+            if 1 <= j <= MODULES:
+                dh_operand = quantise_dh(regrouped_dh[j - 1])
             if j < MODULES:
-                dh_ready[j] = regroup_dh(dh_module)
-                s_ready[j] = quantise_s(s_grouped)
+                regrouped_dh[j] = regroup_dh(dh_module)
+            if 1 <= j <= MODULES:
+                products[j - 1] = multiply(*dh_operand, *quantise_s(regrouped_s[j - 1]))
+            if j >= 2:
+                store(j - 2, products[j - 2])

@@ -15,8 +15,7 @@ MODULES = 8
 UNITS = 512
 FEATURES = 512
 UNIT_TILES = UNITS // P
-CHUNK_SIZES = (1, 1, 2, 2, 2)
-assert sum(CHUNK_SIZES) == MODULES
+CHUNK = 2
 
 FLOPS = 2 * MODULES * UNITS * FEATURES * ROWS
 BYTES = MODULES * ROWS * (2 * FEATURES + 2 * UNITS + 4 * UNITS) + 4 * MODULES * UNITS * FEATURES
@@ -31,7 +30,7 @@ def tile_skill_net_pa_v_kernel(tc, s, ei1, ej1, w11, b11, w12, b12, h, grad_out,
     out_rows = out.rearrange("j (m b) f -> j m b f", b=UNIT_TILES)
 
     with (
-        tc.tile_pool(name="loads", bufs=1) as loads,
+        tc.tile_pool(name="loads", bufs=MODULES // CHUNK) as loads,
         tc.tile_pool(name="grouped", bufs=3) as grouped,
         tc.tile_pool(name="quantised", bufs=2) as quantised,
         tc.tile_pool(name="results", bufs=MODULES) as results,
@@ -39,19 +38,17 @@ def tile_skill_net_pa_v_kernel(tc, s, ei1, ej1, w11, b11, w12, b12, h, grad_out,
         tc.manual_schedule(),
     ):
         s_modules, g_modules, h_modules = [], [], []
-        first = 0
-        for size in CHUNK_SIZES:
-            modules = slice(first, first + size)
-            g_in = loads.tile([P, PACK, size, UNITS], BF16, name="g_in%d" % first)
+        for first in range(0, MODULES, CHUNK):
+            modules = slice(first, first + CHUNK)
+            g_in = loads.tile([P, PACK, CHUNK, UNITS], BF16)
             nc.sync.dma_start(out=g_in[:], in_=g_rows[:, :, modules, :])
-            h_in = loads.tile([P, PACK, size, UNITS], F32, name="h_in%d" % first)
+            h_in = loads.tile([P, PACK, CHUNK, UNITS], F32)
             nc.sync.dma_start(out=h_in[:], in_=h_rows[:, :, modules, :])
-            s_in = loads.tile([P, PACK, size, FEATURES], BF16, name="s_in%d" % first)
+            s_in = loads.tile([P, PACK, CHUNK, FEATURES], BF16)
             nc.sync.dma_start(out=s_in[:], in_=s_rows[:, :, modules, :])
-            g_modules.extend([g_in[:, :, n, :] for n in range(size)])
-            h_modules.extend([h_in[:, :, n, :] for n in range(size)])
-            s_modules.extend([s_in[:, :, n, :] for n in range(size)])
-            first += size
+            g_modules.extend([g_in[:, :, n, :] for n in range(CHUNK)])
+            h_modules.extend([h_in[:, :, n, :] for n in range(CHUNK)])
+            s_modules.extend([s_in[:, :, n, :] for n in range(CHUNK)])
 
         def regroup_s(j):
             s_grouped = grouped.tile([P, FEATURES, PACK], BF16, align_bytes=64)

@@ -15,7 +15,11 @@ MODULES = 8
 UNITS = 512
 FEATURES = 512
 UNIT_TILES = UNITS // P
-CHUNK = 2
+S_CHUNK = 4
+G_CHUNK = 4
+H_CHUNK = 2
+S_MODULES_ON_VECTOR = 5
+SHARED_TAIL = 2
 
 FLOPS = 2 * MODULES * UNITS * FEATURES * ROWS
 BYTES = MODULES * ROWS * (2 * FEATURES + 2 * UNITS + 4 * UNITS) + 4 * MODULES * UNITS * FEATURES
@@ -30,37 +34,58 @@ def tile_skill_net_pa_v_kernel(tc, s, ei1, ej1, w11, b11, w12, b12, h, grad_out,
     out_rows = out.rearrange("j (m b) f -> j m b f", b=UNIT_TILES)
 
     with (
-        tc.tile_pool(name="loads", bufs=MODULES // CHUNK) as loads,
-        tc.tile_pool(name="grouped", bufs=3) as grouped,
-        tc.tile_pool(name="quantised", bufs=2) as quantised,
-        tc.tile_pool(name="results", bufs=MODULES) as results,
+        tc.tile_pool(name="s_loads", bufs=MODULES // S_CHUNK) as s_loads,
+        tc.tile_pool(name="g_loads", bufs=MODULES // G_CHUNK) as g_loads,
+        tc.tile_pool(name="h_loads", bufs=MODULES // H_CHUNK) as h_loads,
+        tc.tile_pool(name="s_grouped_pool", bufs=3) as s_grouped_pool,
+        tc.tile_pool(name="dh_masked_pool", bufs=2) as dh_masked_pool,
+        tc.tile_pool(name="dh_grouped_pool", bufs=3) as dh_grouped_pool,
+        tc.tile_pool(name="s_quantised", bufs=MODULES) as s_quantised,
+        tc.tile_pool(name="dh_quantised", bufs=2) as dh_quantised,
+        tc.tile_pool(name="results", bufs=6) as results,
         tc.psum_pool(name="psum", bufs=8) as psum,
         tc.manual_schedule(),
     ):
-        s_modules, g_modules, h_modules = [], [], []
-        for first in range(0, MODULES, CHUNK):
-            modules = slice(first, first + CHUNK)
-            g_in = loads.tile([P, PACK, CHUNK, UNITS], BF16)
-            nc.sync.dma_start(out=g_in[:], in_=g_rows[:, :, modules, :])
-            h_in = loads.tile([P, PACK, CHUNK, UNITS], F32)
-            nc.sync.dma_start(out=h_in[:], in_=h_rows[:, :, modules, :])
-            s_in = loads.tile([P, PACK, CHUNK, FEATURES], BF16)
-            nc.sync.dma_start(out=s_in[:], in_=s_rows[:, :, modules, :])
-            g_modules.extend([g_in[:, :, n, :] for n in range(CHUNK)])
-            h_modules.extend([h_in[:, :, n, :] for n in range(CHUNK)])
-            s_modules.extend([s_in[:, :, n, :] for n in range(CHUNK)])
+        s_modules, g_modules, h_modules = {}, {}, {}
+
+        def load_s(first):
+            s_in = s_loads.tile([P, PACK, S_CHUNK, FEATURES], BF16)
+            nc.sync.dma_start(out=s_in[:], in_=s_rows[:, :, first : first + S_CHUNK, :])
+            for n in range(S_CHUNK):
+                s_modules[first + n] = s_in[:, :, n, :]
+
+        def load_g(first):
+            g_in = g_loads.tile([P, PACK, G_CHUNK, UNITS], BF16)
+            nc.sync.dma_start(out=g_in[:], in_=g_rows[:, :, first : first + G_CHUNK, :])
+            for n in range(G_CHUNK):
+                g_modules[first + n] = g_in[:, :, n, :]
+
+        def load_h(first):
+            h_in = h_loads.tile([P, PACK, H_CHUNK, UNITS], F32)
+            nc.sync.dma_start(out=h_in[:], in_=h_rows[:, :, first : first + H_CHUNK, :])
+            for n in range(H_CHUNK):
+                h_modules[first + n] = h_in[:, :, n, :]
+
+        for first in range(0, MODULES, S_CHUNK):
+            load_s(first)
+        for first in range(0, MODULES, H_CHUNK):
+            if first % G_CHUNK == 0:
+                load_g(first)
+            load_h(first)
 
         def regroup_s(j):
-            s_grouped = grouped.tile([P, FEATURES, PACK], BF16, align_bytes=64)
-            nc.scalar.copy(
-                out=s_grouped[:].rearrange("p (c i) t -> p c t i", i=4),
-                in_=s_modules[j].rearrange("p t (c i) -> p c t i", i=4),
-            )
+            s_grouped = s_grouped_pool.tile([P, FEATURES, PACK], BF16, align_bytes=64)
+            grouped_view = s_grouped[:].rearrange("p (c i) t -> p c t i", i=4)
+            loaded_view = s_modules[j].rearrange("p t (c i) -> p c t i", i=4)
+            if j < S_MODULES_ON_VECTOR:
+                nc.vector.tensor_copy(out=grouped_view, in_=loaded_view)
+            else:
+                nc.scalar.copy(out=grouped_view, in_=loaded_view)
             return s_grouped
 
         def quantise_s(s_grouped):
-            s_codes = quantised.tile([P, FEATURES], U32, align_bytes=64)
-            s_scales = quantised.tile([P, FEATURES], U8, align_bytes=64)
+            s_codes = s_quantised.tile([P, FEATURES], U32, align_bytes=64)
+            s_scales = s_quantised.tile([P, FEATURES], U8, align_bytes=64)
             nc.vector.quantize_mx(
                 out=s_codes[:].bitcast(E4M3_X4),
                 scales=s_scales[:],
@@ -69,27 +94,30 @@ def tile_skill_net_pa_v_kernel(tc, s, ei1, ej1, w11, b11, w12, b12, h, grad_out,
             return s_codes, s_scales
 
         def mask_dh(j):
+            dh_masked = dh_masked_pool.tile([P, PACK, UNITS], BF16)
             nc.vector.scalar_tensor_tensor(
-                out=g_modules[j],
+                out=dh_masked[:],
                 in0=h_modules[j],
                 scalar=0.0,
                 in1=g_modules[j],
                 op0=ALU.is_gt,
                 op1=ALU.mult,
             )
-            return g_modules[j]
+            return dh_masked[:]
 
-        def regroup_dh(dh_module):
-            dh_grouped = grouped.tile([P, UNIT_TILES, P, PACK], BF16, align_bytes=64)
-            nc.vector.tensor_copy(
-                out=dh_grouped[:].rearrange("p b m t -> p m t b"),
-                in_=dh_module.rearrange("p t (m b) -> p m t b", b=UNIT_TILES),
-            )
+        def regroup_dh(j, dh_module):
+            dh_grouped = dh_grouped_pool.tile([P, UNIT_TILES, P, PACK], BF16, align_bytes=64)
+            grouped_view = dh_grouped[:].rearrange("p b m t -> p m t b")
+            masked_view = dh_module.rearrange("p t (m b) -> p m t b", b=UNIT_TILES)
+            if j % 2 == 0:
+                nc.scalar.copy(out=grouped_view, in_=masked_view)
+            else:
+                nc.vector.tensor_copy(out=grouped_view, in_=masked_view)
             return dh_grouped
 
         def quantise_dh(dh_grouped):
-            dh_codes = quantised.tile([P, UNITS], U32, align_bytes=64)
-            dh_scales = quantised.tile([P, UNITS], U8, align_bytes=64)
+            dh_codes = dh_quantised.tile([P, UNITS], U32, align_bytes=64)
+            dh_scales = dh_quantised.tile([P, UNITS], U8, align_bytes=64)
             nc.vector.quantize_mx(
                 out=dh_codes[:].bitcast(E5M2_X4),
                 scales=dh_scales[:],
@@ -117,19 +145,28 @@ def tile_skill_net_pa_v_kernel(tc, s, ei1, ej1, w11, b11, w12, b12, h, grad_out,
         def store(j, banks):
             result = results.tile([P, UNIT_TILES, FEATURES], F32)
             for b in range(UNIT_TILES):
-                nc.scalar.copy(out=result[:, b, :], in_=banks[b][:])
+                if j >= MODULES - SHARED_TAIL and b % 2 == 1:
+                    nc.vector.tensor_copy(out=result[:, b, :], in_=banks[b][:])
+                else:
+                    nc.scalar.copy(out=result[:, b, :], in_=banks[b][:])
             nc.sync.dma_start(out=out_rows[j], in_=result[:])
 
-        regrouped_s, regrouped_dh, products = {}, {}, {}
-        for j in range(MODULES + 2):
+        regrouped_s, s_operands = {}, {}
+        for j in range(MODULES + 1):
             if j < MODULES:
                 regrouped_s[j] = regroup_s(j)
+            if j >= 1:
+                s_operands[j - 1] = quantise_s(regrouped_s[j - 1])
+
+        regrouped_dh, products = {}, {}
+        for j in range(MODULES + 2):
+            if j < MODULES:
                 dh_module = mask_dh(j)
             if 1 <= j <= MODULES:
                 dh_operand = quantise_dh(regrouped_dh[j - 1])
-            if j < MODULES:
-                regrouped_dh[j] = regroup_dh(dh_module)
-            if 1 <= j <= MODULES:
-                products[j - 1] = multiply(*dh_operand, *quantise_s(regrouped_s[j - 1]))
             if j >= 2:
                 store(j - 2, products[j - 2])
+            if j < MODULES:
+                regrouped_dh[j] = regroup_dh(j, dh_module)
+            if 1 <= j <= MODULES:
+                products[j - 1] = multiply(*dh_operand, *s_operands[j - 1])

@@ -16,9 +16,10 @@ UNITS = 512
 FEATURES = 512
 UNIT_TILES = UNITS // P
 S_CHUNK = 4
-G_CHUNK = 4
+G_CHUNKS = (2, 2, 2, 2)
 H_CHUNK = 2
-S_MODULES_ON_VECTOR = 5
+S_MODULES_OF_A_CHUNK_ON_VECTOR = 2
+DH_MODULES_ON_SCALAR = (0, 1, 3, 5)
 SHARED_TAIL = 2
 
 FLOPS = 2 * MODULES * UNITS * FEATURES * ROWS
@@ -35,7 +36,7 @@ def tile_skill_net_pa_v_kernel(tc, s, ei1, ej1, w11, b11, w12, b12, h, grad_out,
 
     with (
         tc.tile_pool(name="s_loads", bufs=MODULES // S_CHUNK) as s_loads,
-        tc.tile_pool(name="g_loads", bufs=MODULES // G_CHUNK) as g_loads,
+        tc.tile_pool(name="g_loads", bufs=1) as g_loads,
         tc.tile_pool(name="h_loads", bufs=MODULES // H_CHUNK) as h_loads,
         tc.tile_pool(name="s_grouped_pool", bufs=3) as s_grouped_pool,
         tc.tile_pool(name="dh_masked_pool", bufs=2) as dh_masked_pool,
@@ -54,10 +55,10 @@ def tile_skill_net_pa_v_kernel(tc, s, ei1, ej1, w11, b11, w12, b12, h, grad_out,
             for n in range(S_CHUNK):
                 s_modules[first + n] = s_in[:, :, n, :]
 
-        def load_g(first):
-            g_in = g_loads.tile([P, PACK, G_CHUNK, UNITS], BF16)
-            nc.sync.dma_start(out=g_in[:], in_=g_rows[:, :, first : first + G_CHUNK, :])
-            for n in range(G_CHUNK):
+        def load_g(first, count):
+            g_in = g_loads.tile([P, PACK, count, UNITS], BF16, name="g_in_%d" % first)
+            nc.sync.dma_start(out=g_in[:], in_=g_rows[:, :, first : first + count, :])
+            for n in range(count):
                 g_modules[first + n] = g_in[:, :, n, :]
 
         def load_h(first):
@@ -68,16 +69,17 @@ def tile_skill_net_pa_v_kernel(tc, s, ei1, ej1, w11, b11, w12, b12, h, grad_out,
 
         for first in range(0, MODULES, S_CHUNK):
             load_s(first)
+        g_firsts = {sum(G_CHUNKS[:n]): G_CHUNKS[n] for n in range(len(G_CHUNKS))}
         for first in range(0, MODULES, H_CHUNK):
-            if first % G_CHUNK == 0:
-                load_g(first)
+            if first in g_firsts:
+                load_g(first, g_firsts[first])
             load_h(first)
 
         def regroup_s(j):
             s_grouped = s_grouped_pool.tile([P, FEATURES, PACK], BF16, align_bytes=64)
             grouped_view = s_grouped[:].rearrange("p (c i) t -> p c t i", i=4)
             loaded_view = s_modules[j].rearrange("p t (c i) -> p c t i", i=4)
-            if j < S_MODULES_ON_VECTOR:
+            if j % S_CHUNK < S_MODULES_OF_A_CHUNK_ON_VECTOR:
                 nc.vector.tensor_copy(out=grouped_view, in_=loaded_view)
             else:
                 nc.scalar.copy(out=grouped_view, in_=loaded_view)
@@ -109,7 +111,7 @@ def tile_skill_net_pa_v_kernel(tc, s, ei1, ej1, w11, b11, w12, b12, h, grad_out,
             dh_grouped = dh_grouped_pool.tile([P, UNIT_TILES, P, PACK], BF16, align_bytes=64)
             grouped_view = dh_grouped[:].rearrange("p b m t -> p m t b")
             masked_view = dh_module.rearrange("p t (m b) -> p m t b", b=UNIT_TILES)
-            if j % 2 == 0:
+            if j in DH_MODULES_ON_SCALAR:
                 nc.scalar.copy(out=grouped_view, in_=masked_view)
             else:
                 nc.vector.tensor_copy(out=grouped_view, in_=masked_view)

@@ -16,10 +16,10 @@ UNITS = 512
 FEATURES = 512
 UNIT_TILES = UNITS // P
 S_CHUNK = 4
-G_CHUNKS = (2, 2, 2, 2)
+G_CHUNK = 4
 H_CHUNK = 2
 S_MODULES_OF_A_CHUNK_ON_VECTOR = 2
-DH_MODULES_ON_SCALAR = (0, 1, 3, 5)
+DH_MODULES_ON_SCALAR = (1, 3, 5)
 SHARED_TAIL = 2
 
 FLOPS = 2 * MODULES * UNITS * FEATURES * ROWS
@@ -36,11 +36,11 @@ def tile_skill_net_pa_v_kernel(tc, s, ei1, ej1, w11, b11, w12, b12, h, grad_out,
 
     with (
         tc.tile_pool(name="s_loads", bufs=MODULES // S_CHUNK) as s_loads,
-        tc.tile_pool(name="g_loads", bufs=1) as g_loads,
+        tc.tile_pool(name="g_loads", bufs=MODULES // G_CHUNK) as g_loads,
         tc.tile_pool(name="h_loads", bufs=MODULES // H_CHUNK) as h_loads,
         tc.tile_pool(name="s_grouped_pool", bufs=3) as s_grouped_pool,
-        tc.tile_pool(name="dh_masked_pool", bufs=2) as dh_masked_pool,
-        tc.tile_pool(name="dh_grouped_pool", bufs=3) as dh_grouped_pool,
+        tc.tile_pool(name="dh_masked_pool", bufs=3) as dh_masked_pool,
+        tc.tile_pool(name="dh_grouped_pool", bufs=2) as dh_grouped_pool,
         tc.tile_pool(name="s_quantised", bufs=MODULES) as s_quantised,
         tc.tile_pool(name="dh_quantised", bufs=2) as dh_quantised,
         tc.tile_pool(name="results", bufs=6) as results,
@@ -55,10 +55,10 @@ def tile_skill_net_pa_v_kernel(tc, s, ei1, ej1, w11, b11, w12, b12, h, grad_out,
             for n in range(S_CHUNK):
                 s_modules[first + n] = s_in[:, :, n, :]
 
-        def load_g(first, count):
-            g_in = g_loads.tile([P, PACK, count, UNITS], BF16, name="g_in_%d" % first)
-            nc.sync.dma_start(out=g_in[:], in_=g_rows[:, :, first : first + count, :])
-            for n in range(count):
+        def load_g(first):
+            g_in = g_loads.tile([P, PACK, G_CHUNK, UNITS], BF16)
+            nc.sync.dma_start(out=g_in[:], in_=g_rows[:, :, first : first + G_CHUNK, :])
+            for n in range(G_CHUNK):
                 g_modules[first + n] = g_in[:, :, n, :]
 
         def load_h(first):
@@ -69,11 +69,10 @@ def tile_skill_net_pa_v_kernel(tc, s, ei1, ej1, w11, b11, w12, b12, h, grad_out,
 
         for first in range(0, MODULES, S_CHUNK):
             load_s(first)
-        g_firsts = {sum(G_CHUNKS[:n]): G_CHUNKS[n] for n in range(len(G_CHUNKS))}
         for first in range(0, MODULES, H_CHUNK):
-            if first in g_firsts:
-                load_g(first, g_firsts[first])
             load_h(first)
+            if first % G_CHUNK == 0:
+                load_g(first)
 
         def regroup_s(j):
             s_grouped = s_grouped_pool.tile([P, FEATURES, PACK], BF16, align_bytes=64)
@@ -95,17 +94,14 @@ def tile_skill_net_pa_v_kernel(tc, s, ei1, ej1, w11, b11, w12, b12, h, grad_out,
             )
             return s_codes, s_scales
 
-        def mask_dh(j):
-            dh_masked = dh_masked_pool.tile([P, PACK, UNITS], BF16)
-            nc.vector.scalar_tensor_tensor(
-                out=dh_masked[:],
-                in0=h_modules[j],
-                scalar=0.0,
-                in1=g_modules[j],
-                op0=ALU.is_gt,
-                op1=ALU.mult,
-            )
-            return dh_masked[:]
+        def make_mask(j):
+            mask = dh_masked_pool.tile([P, PACK, UNITS], BF16)
+            nc.vector.tensor_scalar(out=mask[:], in0=h_modules[j], scalar1=0.0, scalar2=None, op0=ALU.is_gt)
+            return mask
+
+        def mask_dh(j, mask):
+            nc.vector.tensor_tensor(out=mask[:], in0=mask[:], in1=g_modules[j], op=ALU.mult)
+            return mask[:]
 
         def regroup_dh(j, dh_module):
             dh_grouped = dh_grouped_pool.tile([P, UNIT_TILES, P, PACK], BF16, align_bytes=64)
@@ -160,10 +156,13 @@ def tile_skill_net_pa_v_kernel(tc, s, ei1, ej1, w11, b11, w12, b12, h, grad_out,
             if j >= 1:
                 s_operands[j - 1] = quantise_s(regrouped_s[j - 1])
 
-        regrouped_dh, products = {}, {}
+        mask_tiles, regrouped_dh, products = {}, {}, {}
         for j in range(MODULES + 2):
+            if j < MODULES and j % H_CHUNK == 0:
+                for n in range(H_CHUNK):
+                    mask_tiles[j + n] = make_mask(j + n)
             if j < MODULES:
-                dh_module = mask_dh(j)
+                dh_module = mask_dh(j, mask_tiles[j])
             if 1 <= j <= MODULES:
                 dh_operand = quantise_dh(regrouped_dh[j - 1])
             if j >= 2:

@@ -15,11 +15,12 @@ MODULES = 8
 UNITS = 512
 FEATURES = 512
 UNIT_TILES = UNITS // P
-S_CHUNK = 4
+S_CHUNK = 8
 G_CHUNK = 4
 H_CHUNK = 2
-S_MODULES_OF_A_CHUNK_ON_VECTOR = 2
-DH_MODULES_ON_SCALAR = (1, 3, 5)
+S_MODULES_ON_VECTOR = 3
+S_MODULES_QUANTISED_LATE = 3
+DH_MODULES_ON_SCALAR = (1, 2, 3, 5)
 SHARED_TAIL = 2
 
 FLOPS = 2 * MODULES * UNITS * FEATURES * ROWS
@@ -38,12 +39,13 @@ def tile_skill_net_pa_v_kernel(tc, s, ei1, ej1, w11, b11, w12, b12, h, grad_out,
         tc.tile_pool(name="s_loads", bufs=MODULES // S_CHUNK) as s_loads,
         tc.tile_pool(name="g_loads", bufs=MODULES // G_CHUNK) as g_loads,
         tc.tile_pool(name="h_loads", bufs=MODULES // H_CHUNK) as h_loads,
-        tc.tile_pool(name="s_grouped_pool", bufs=3) as s_grouped_pool,
+        tc.tile_pool(name="s_grouped_by_vector", bufs=2) as s_grouped_by_vector,
+        tc.tile_pool(name="s_grouped_by_scalar", bufs=3) as s_grouped_by_scalar,
         tc.tile_pool(name="dh_masked_pool", bufs=3) as dh_masked_pool,
         tc.tile_pool(name="dh_grouped_pool", bufs=2) as dh_grouped_pool,
         tc.tile_pool(name="s_quantised", bufs=MODULES) as s_quantised,
         tc.tile_pool(name="dh_quantised", bufs=2) as dh_quantised,
-        tc.tile_pool(name="results", bufs=6) as results,
+        tc.tile_pool(name="results", bufs=5) as results,
         tc.psum_pool(name="psum", bufs=8) as psum,
         tc.manual_schedule(),
     ):
@@ -75,10 +77,12 @@ def tile_skill_net_pa_v_kernel(tc, s, ei1, ej1, w11, b11, w12, b12, h, grad_out,
                 load_g(first)
 
         def regroup_s(j):
-            s_grouped = s_grouped_pool.tile([P, FEATURES, PACK], BF16, align_bytes=64)
+            on_vector = j < S_MODULES_ON_VECTOR
+            pool = s_grouped_by_vector if on_vector else s_grouped_by_scalar
+            s_grouped = pool.tile([P, FEATURES, PACK], BF16, align_bytes=64)
             grouped_view = s_grouped[:].rearrange("p (c i) t -> p c t i", i=4)
             loaded_view = s_modules[j].rearrange("p t (c i) -> p c t i", i=4)
-            if j % S_CHUNK < S_MODULES_OF_A_CHUNK_ON_VECTOR:
+            if on_vector:
                 nc.vector.tensor_copy(out=grouped_view, in_=loaded_view)
             else:
                 nc.scalar.copy(out=grouped_view, in_=loaded_view)
@@ -153,7 +157,7 @@ def tile_skill_net_pa_v_kernel(tc, s, ei1, ej1, w11, b11, w12, b12, h, grad_out,
         for j in range(MODULES + 1):
             if j < MODULES:
                 regrouped_s[j] = regroup_s(j)
-            if j >= 1:
+            if 1 <= j <= MODULES - S_MODULES_QUANTISED_LATE:
                 s_operands[j - 1] = quantise_s(regrouped_s[j - 1])
 
         mask_tiles, regrouped_dh, products = {}, {}, {}
@@ -169,5 +173,8 @@ def tile_skill_net_pa_v_kernel(tc, s, ei1, ej1, w11, b11, w12, b12, h, grad_out,
                 store(j - 2, products[j - 2])
             if j < MODULES:
                 regrouped_dh[j] = regroup_dh(j, dh_module)
+            if 1 <= j <= S_MODULES_QUANTISED_LATE:
+                late = MODULES - S_MODULES_QUANTISED_LATE + j - 1
+                s_operands[late] = quantise_s(regrouped_s[late])
             if 1 <= j <= MODULES:
                 products[j - 1] = multiply(*dh_operand, *s_operands[j - 1])

@@ -1,4 +1,5 @@
 import concourse.mybir as mybir
+from concourse.masks import make_identity
 
 BF16 = mybir.dt.bfloat16
 F32 = mybir.dt.float32
@@ -10,22 +11,24 @@ ALU = mybir.AluOpType
 
 P = 128
 PACK = 4
+HALF = PACK // 2
 ROWS = P * PACK
 MODULES = 8
 UNITS = 512
 FEATURES = 512
 UNIT_TILES = UNITS // P
-S_CHUNK = 8
-G_CHUNK = 4
-H_CHUNK = 2
-S_MODULES_ON_VECTOR = 3
-S_MODULES_QUANTISED_LATE = 3
-DH_MODULES_ON_SCALAR = (1, 2, 3, 5)
+H_CHUNKS = ((0, 1), (2, 3, 4), (5, 6, 7))
+S_BY_VECTOR = (0, 1, 2, 3)
+S_BY_SCALAR_IN_HALVES = (4, 5, 6)
+S_BY_SCALAR_WHOLE = (7,)
+G_BY_TENSOR = (0, 1, 2)
+G_BY_SCALAR = (3, 4, 5)
+G_BY_VECTOR = (6, 7)
 SHARED_TAIL = 2
+RESULT_GROUP = 4
 
 FLOPS = 2 * MODULES * UNITS * FEATURES * ROWS
 BYTES = MODULES * ROWS * (2 * FEATURES + 2 * UNITS + 4 * UNITS) + 4 * MODULES * UNITS * FEATURES
-
 
 def tile_skill_net_pa_v_kernel(tc, s, ei1, ej1, w11, b11, w12, b12, h, grad_out, out):
     nc = tc.nc
@@ -36,57 +39,60 @@ def tile_skill_net_pa_v_kernel(tc, s, ei1, ej1, w11, b11, w12, b12, h, grad_out,
     out_rows = out.rearrange("j (m b) f -> j m b f", b=UNIT_TILES)
 
     with (
-        tc.tile_pool(name="s_loads", bufs=MODULES // S_CHUNK) as s_loads,
-        tc.tile_pool(name="g_loads", bufs=MODULES // G_CHUNK) as g_loads,
-        tc.tile_pool(name="h_loads", bufs=MODULES // H_CHUNK) as h_loads,
-        tc.tile_pool(name="s_grouped_by_vector", bufs=2) as s_grouped_by_vector,
-        tc.tile_pool(name="s_grouped_by_scalar", bufs=3) as s_grouped_by_scalar,
-        tc.tile_pool(name="dh_masked_pool", bufs=3) as dh_masked_pool,
-        tc.tile_pool(name="dh_grouped_pool", bufs=2) as dh_grouped_pool,
+        tc.tile_pool(name="constants", bufs=1) as constants,
+        tc.tile_pool(name="s_space", bufs=1) as s_space,
+        tc.tile_pool(name="g_space", bufs=1) as g_space,
+        tc.tile_pool(name="h_loads", bufs=1) as h_loads,
+        tc.tile_pool(name="s_grouped_by_vector", bufs=4) as s_grouped_by_vector,
+        tc.tile_pool(name="s_grouped_by_scalar", bufs=4) as s_grouped_by_scalar,
+        tc.tile_pool(name="g_grouped_pool", bufs=len(G_BY_SCALAR) + len(G_BY_VECTOR)) as g_grouped_pool,
+        tc.tile_pool(name="dh_pool", bufs=4) as dh_pool,
         tc.tile_pool(name="s_quantised", bufs=MODULES) as s_quantised,
         tc.tile_pool(name="dh_quantised", bufs=2) as dh_quantised,
-        tc.tile_pool(name="results", bufs=5) as results,
         tc.psum_pool(name="psum", bufs=8) as psum,
         tc.manual_schedule(),
     ):
-        s_modules, g_modules, h_modules = {}, {}, {}
+        identity = constants.tile([P, P], BF16)
+        make_identity(nc, identity[:])
 
-        def load_s(first):
-            s_in = s_loads.tile([P, PACK, S_CHUNK, FEATURES], BF16)
-            nc.sync.dma_start(out=s_in[:], in_=s_rows[:, :, first : first + S_CHUNK, :])
-            for n in range(S_CHUNK):
-                s_modules[first + n] = s_in[:, :, n, :]
+        s_in = s_space.tile([P, PACK, MODULES, FEATURES], BF16, name="s_bytes")
+        for first in range(0, PACK, HALF):
+            rows = slice(first, first + HALF)
+            nc.sync.dma_start(out=s_in[:, rows], in_=s_rows[:, rows])
 
-        def load_g(first):
-            g_in = g_loads.tile([P, PACK, G_CHUNK, UNITS], BF16)
-            nc.sync.dma_start(out=g_in[:], in_=g_rows[:, :, first : first + G_CHUNK, :])
-            for n in range(G_CHUNK):
-                g_modules[first + n] = g_in[:, :, n, :]
+        h_modules = {}
 
-        def load_h(first):
-            h_in = h_loads.tile([P, PACK, H_CHUNK, UNITS], F32)
-            nc.sync.dma_start(out=h_in[:], in_=h_rows[:, :, first : first + H_CHUNK, :])
-            for n in range(H_CHUNK):
+        def load_h(chunk):
+            first, count = chunk[0], len(chunk)
+            h_in = h_loads.tile([P, PACK, count, UNITS], F32, name="h_in_%d" % first)
+            nc.sync.dma_start(out=h_in[:], in_=h_rows[:, :, first : first + count, :])
+            for n in range(count):
                 h_modules[first + n] = h_in[:, :, n, :]
 
-        for first in range(0, MODULES, S_CHUNK):
-            load_s(first)
-        for first in range(0, MODULES, H_CHUNK):
-            load_h(first)
-            if first % G_CHUNK == 0:
-                load_g(first)
+        load_h(H_CHUNKS[0])
+        g_in = g_space.tile([P, PACK, MODULES, UNITS], BF16, name="g_bytes")
+        for first in range(0, PACK, HALF):
+            rows = slice(first, first + HALF)
+            nc.sync.dma_start(out=g_in[:, rows], in_=g_rows[:, rows])
+        for chunk in H_CHUNKS[1:]:
+            load_h(chunk)
 
-        def regroup_s(j):
-            on_vector = j < S_MODULES_ON_VECTOR
-            pool = s_grouped_by_vector if on_vector else s_grouped_by_scalar
-            s_grouped = pool.tile([P, FEATURES, PACK], BF16, align_bytes=64)
-            grouped_view = s_grouped[:].rearrange("p (c i) t -> p c t i", i=4)
-            loaded_view = s_modules[j].rearrange("p t (c i) -> p c t i", i=4)
-            if on_vector:
-                nc.vector.tensor_copy(out=grouped_view, in_=loaded_view)
+        first_half, second_half, whole = slice(0, HALF), slice(HALF, PACK), slice(0, PACK)
+
+        def regroup_s(copy, j, s_grouped, rows):
+            if rows == whole:
+                grouped_view = s_grouped[:].rearrange("p (c i) t -> p c t i", i=4)
+                loaded_view = s_in[:, :, j, :].rearrange("p t (c i) -> p c t i", i=4)
             else:
-                nc.scalar.copy(out=grouped_view, in_=loaded_view)
-            return s_grouped
+                grouped_view = s_grouped[:, :, rows]
+                loaded_view = s_in[:, rows, j, :].rearrange("p t f -> p f t")
+            copy(out=grouped_view, in_=loaded_view)
+
+        def regroup_g(copy, j, g_grouped, rows):
+            copy(
+                out=g_grouped[:, :, :, rows].rearrange("p b m t -> p m t b"),
+                in_=g_in[:, rows, j, :].rearrange("p t (m b) -> p m t b", b=UNIT_TILES),
+            )
 
         def quantise_s(s_grouped):
             s_codes = s_quantised.tile([P, FEATURES], U32, align_bytes=64)
@@ -99,23 +105,39 @@ def tile_skill_net_pa_v_kernel(tc, s, ei1, ej1, w11, b11, w12, b12, h, grad_out,
             return s_codes, s_scales
 
         def make_mask(j):
-            mask = dh_masked_pool.tile([P, PACK, UNITS], BF16)
-            nc.vector.tensor_scalar(out=mask[:], in0=h_modules[j], scalar1=0.0, scalar2=None, op0=ALU.is_gt)
+            mask = dh_pool.tile([P, UNIT_TILES, P, PACK], BF16, align_bytes=64)
+            nc.vector.tensor_scalar(
+                out=mask[:].rearrange("p b m t -> p m t b"),
+                in0=h_modules[j].rearrange("p t (m b) -> p m t b", b=UNIT_TILES),
+                scalar1=0.0,
+                scalar2=None,
+                op0=ALU.is_gt,
+            )
             return mask
 
-        def mask_dh(j, mask):
-            nc.vector.tensor_tensor(out=mask[:], in0=mask[:], in1=g_modules[j], op=ALU.mult)
-            return mask[:]
+        def regroup_g_by_tensor(j):
+            banks = []
+            loaded_view = g_in[:, :, j, :].rearrange("p t (m b) -> p b m t", b=UNIT_TILES)
+            for first in range(0, UNIT_TILES, 2):
+                acc = psum.tile([P, 2, P, PACK], BF16)
+                for n in range(2):
+                    nc.tensor.matmul(
+                        out=acc[:, n],
+                        lhsT=identity[:],
+                        rhs=loaded_view[:, first + n],
+                        start=True,
+                        stop=True,
+                    )
+                banks.append(acc)
+            return banks
 
-        def regroup_dh(j, dh_module):
-            dh_grouped = dh_grouped_pool.tile([P, UNIT_TILES, P, PACK], BF16, align_bytes=64)
-            grouped_view = dh_grouped[:].rearrange("p b m t -> p m t b")
-            masked_view = dh_module.rearrange("p t (m b) -> p m t b", b=UNIT_TILES)
-            if j in DH_MODULES_ON_SCALAR:
-                nc.scalar.copy(out=grouped_view, in_=masked_view)
+        def mask_dh(j, mask):
+            if j in G_BY_TENSOR:
+                for n, bank in enumerate(g_operands[j]):
+                    part = mask[:, 2 * n : 2 * n + 2]
+                    nc.vector.tensor_tensor(out=part, in0=part, in1=bank[:], op=ALU.mult)
             else:
-                nc.vector.tensor_copy(out=grouped_view, in_=masked_view)
-            return dh_grouped
+                nc.vector.tensor_tensor(out=mask[:], in0=mask[:], in1=g_operands[j][:], op=ALU.mult)
 
         def quantise_dh(dh_grouped):
             dh_codes = dh_quantised.tile([P, UNITS], U32, align_bytes=64)
@@ -144,37 +166,74 @@ def tile_skill_net_pa_v_kernel(tc, s, ei1, ej1, w11, b11, w12, b12, h, grad_out,
                 banks.append(acc)
             return banks
 
+        result_groups = {}
+
         def store(j, banks):
-            result = results.tile([P, UNIT_TILES, FEATURES], F32)
+            group, place = divmod(j, RESULT_GROUP)
+            if place == 0:
+                space, name = (s_space, "s_bytes") if group == 0 else (g_space, "g_bytes")
+                result_groups[group] = space.tile([P, RESULT_GROUP, UNIT_TILES, FEATURES], F32, name=name)
+            result = result_groups[group][:, place]
             for b in range(UNIT_TILES):
                 if j >= MODULES - SHARED_TAIL and b % 2 == 1:
                     nc.vector.tensor_copy(out=result[:, b, :], in_=banks[b][:])
                 else:
                     nc.scalar.copy(out=result[:, b, :], in_=banks[b][:])
-            nc.sync.dma_start(out=out_rows[j], in_=result[:])
+            nc.sync.dma_start(out=out_rows[j], in_=result)
 
-        regrouped_s, s_operands = {}, {}
+        s_tiles, s_operands = {}, {}
+        for j in S_BY_VECTOR:
+            s_grouped = s_grouped_by_vector.tile([P, FEATURES, PACK], BF16, align_bytes=64)
+            s_tiles[j] = s_grouped
+            regroup_s(nc.vector.tensor_copy, j, s_grouped, first_half)
+        for j in S_BY_SCALAR_IN_HALVES + S_BY_SCALAR_WHOLE:
+            s_grouped = s_grouped_by_scalar.tile([P, FEATURES, PACK], BF16, align_bytes=64)
+            s_tiles[j] = s_grouped
+            if j in S_BY_SCALAR_IN_HALVES:
+                regroup_s(nc.scalar.copy, j, s_grouped, first_half)
+        for j in S_BY_SCALAR_IN_HALVES:
+            regroup_s(nc.scalar.copy, j, s_tiles[j], second_half)
+        for j in S_BY_SCALAR_WHOLE:
+            regroup_s(nc.scalar.copy, j, s_tiles[j], whole)
         for j in range(MODULES + 1):
-            if j < MODULES:
-                regrouped_s[j] = regroup_s(j)
-            if 1 <= j <= MODULES - S_MODULES_QUANTISED_LATE:
-                s_operands[j - 1] = quantise_s(regrouped_s[j - 1])
+            if j in S_BY_VECTOR:
+                regroup_s(nc.vector.tensor_copy, j, s_tiles[j], second_half)
+            if j >= 1:
+                s_operands[j - 1] = quantise_s(s_tiles[j - 1])
 
-        mask_tiles, regrouped_dh, products = {}, {}, {}
-        for j in range(MODULES + 2):
-            if j < MODULES and j % H_CHUNK == 0:
-                for n in range(H_CHUNK):
-                    mask_tiles[j + n] = make_mask(j + n)
-            if j < MODULES:
-                dh_module = mask_dh(j, mask_tiles[j])
-            if 1 <= j <= MODULES:
-                dh_operand = quantise_dh(regrouped_dh[j - 1])
-            if j >= 2:
-                store(j - 2, products[j - 2])
-            if j < MODULES:
-                regrouped_dh[j] = regroup_dh(j, dh_module)
-            if 1 <= j <= S_MODULES_QUANTISED_LATE:
-                late = MODULES - S_MODULES_QUANTISED_LATE + j - 1
-                s_operands[late] = quantise_s(regrouped_s[late])
-            if 1 <= j <= MODULES:
-                products[j - 1] = multiply(*dh_operand, *s_operands[j - 1])
+        mask_tiles, g_operands, products = {}, {}, {}
+        for j in H_CHUNKS[0]:
+            mask_tiles[j] = make_mask(j)
+        for rows in (first_half, second_half):
+            for j in G_BY_SCALAR:
+                if rows == first_half:
+                    g_grouped = g_grouped_pool.tile([P, UNIT_TILES, P, PACK], BF16, align_bytes=64)
+                    g_operands[j] = g_grouped
+                regroup_g(nc.scalar.copy, j, g_operands[j], rows)
+        for j in G_BY_VECTOR:
+            g_grouped = g_grouped_pool.tile([P, UNIT_TILES, P, PACK], BF16, align_bytes=64)
+            g_operands[j] = g_grouped
+            regroup_g(nc.vector.tensor_copy, j, g_grouped, first_half)
+
+        def finish(j):
+            products[j] = multiply(*quantise_dh(mask_tiles[j]), *s_operands[j])
+
+        for j in H_CHUNKS[0]:
+            g_operands[j] = regroup_g_by_tensor(j)
+        for j in H_CHUNKS[0]:
+            mask_dh(j, mask_tiles[j])
+        for j in H_CHUNKS[0]:
+            finish(j)
+        g_operands[2] = regroup_g_by_tensor(2)
+        for j in G_BY_VECTOR:
+            regroup_g(nc.vector.tensor_copy, j, g_operands[j], second_half)
+
+        for j in range(2, MODULES):
+            mask_tiles[j] = make_mask(j)
+            if j > 2:
+                finish(j - 1)
+            mask_dh(j, mask_tiles[j])
+            store(j - 2, products[j - 2])
+        finish(MODULES - 1)
+        for j in range(MODULES - SHARED_TAIL, MODULES):
+            store(j, products[j])

@@ -11,7 +11,6 @@ ALU = mybir.AluOpType
 
 P = 128
 PACK = 4
-HALF = PACK // 2
 ROWS = P * PACK
 MODULES = 8
 UNITS = 512
@@ -19,8 +18,7 @@ FEATURES = 512
 UNIT_TILES = UNITS // P
 H_CHUNKS = ((0, 1), (2, 3, 4), (5, 6, 7))
 S_BY_VECTOR = (0, 1, 2, 3)
-S_BY_SCALAR_IN_HALVES = (4, 5, 6)
-S_BY_SCALAR_WHOLE = (7,)
+S_BY_SCALAR = (4, 5, 6, 7)
 G_BY_TENSOR = (0, 1, 2)
 G_BY_SCALAR = (3, 4, 5)
 G_BY_VECTOR = (6, 7)
@@ -56,9 +54,7 @@ def tile_skill_net_pa_v_kernel(tc, s, ei1, ej1, w11, b11, w12, b12, h, grad_out,
         make_identity(nc, identity[:])
 
         s_in = s_space.tile([P, PACK, MODULES, FEATURES], BF16, name="s_bytes")
-        for first in range(0, PACK, HALF):
-            rows = slice(first, first + HALF)
-            nc.sync.dma_start(out=s_in[:, rows], in_=s_rows[:, rows])
+        nc.sync.dma_start(out=s_in[:], in_=s_rows)
 
         h_modules = {}
 
@@ -71,27 +67,20 @@ def tile_skill_net_pa_v_kernel(tc, s, ei1, ej1, w11, b11, w12, b12, h, grad_out,
 
         load_h(H_CHUNKS[0])
         g_in = g_space.tile([P, PACK, MODULES, UNITS], BF16, name="g_bytes")
-        for first in range(0, PACK, HALF):
-            rows = slice(first, first + HALF)
-            nc.sync.dma_start(out=g_in[:, rows], in_=g_rows[:, rows])
+        nc.sync.dma_start(out=g_in[:], in_=g_rows)
         for chunk in H_CHUNKS[1:]:
             load_h(chunk)
 
-        first_half, second_half, whole = slice(0, HALF), slice(HALF, PACK), slice(0, PACK)
-
-        def regroup_s(copy, j, s_grouped, rows):
-            if rows == whole:
-                grouped_view = s_grouped[:].rearrange("p (c i) t -> p c t i", i=4)
-                loaded_view = s_in[:, :, j, :].rearrange("p t (c i) -> p c t i", i=4)
-            else:
-                grouped_view = s_grouped[:, :, rows]
-                loaded_view = s_in[:, rows, j, :].rearrange("p t f -> p f t")
-            copy(out=grouped_view, in_=loaded_view)
-
-        def regroup_g(copy, j, g_grouped, rows):
+        def regroup_s(copy, j, s_grouped):
             copy(
-                out=g_grouped[:, :, :, rows].rearrange("p b m t -> p m t b"),
-                in_=g_in[:, rows, j, :].rearrange("p t (m b) -> p m t b", b=UNIT_TILES),
+                out=s_grouped[:].rearrange("p (c i) t -> p c t i", i=4),
+                in_=s_in[:, :, j, :].rearrange("p t (c i) -> p c t i", i=4),
+            )
+
+        def regroup_g(copy, j, g_grouped):
+            copy(
+                out=g_grouped[:].rearrange("p b m t -> p m t b"),
+                in_=g_in[:, :, j, :].rearrange("p t (m b) -> p m t b", b=UNIT_TILES),
             )
 
         def quantise_s(s_grouped):
@@ -182,38 +171,25 @@ def tile_skill_net_pa_v_kernel(tc, s, ei1, ej1, w11, b11, w12, b12, h, grad_out,
             nc.sync.dma_start(out=out_rows[j], in_=result)
 
         s_tiles, s_operands = {}, {}
-        for j in S_BY_VECTOR:
-            s_grouped = s_grouped_by_vector.tile([P, FEATURES, PACK], BF16, align_bytes=64)
-            s_tiles[j] = s_grouped
-            regroup_s(nc.vector.tensor_copy, j, s_grouped, first_half)
-        for j in S_BY_SCALAR_IN_HALVES + S_BY_SCALAR_WHOLE:
+        for j in S_BY_SCALAR:
             s_grouped = s_grouped_by_scalar.tile([P, FEATURES, PACK], BF16, align_bytes=64)
             s_tiles[j] = s_grouped
-            if j in S_BY_SCALAR_IN_HALVES:
-                regroup_s(nc.scalar.copy, j, s_grouped, first_half)
-        for j in S_BY_SCALAR_IN_HALVES:
-            regroup_s(nc.scalar.copy, j, s_tiles[j], second_half)
-        for j in S_BY_SCALAR_WHOLE:
-            regroup_s(nc.scalar.copy, j, s_tiles[j], whole)
+            regroup_s(nc.scalar.copy, j, s_grouped)
         for j in range(MODULES + 1):
             if j in S_BY_VECTOR:
-                regroup_s(nc.vector.tensor_copy, j, s_tiles[j], second_half)
+                s_grouped = s_grouped_by_vector.tile([P, FEATURES, PACK], BF16, align_bytes=64)
+                s_tiles[j] = s_grouped
+                regroup_s(nc.vector.tensor_copy, j, s_grouped)
             if j >= 1:
                 s_operands[j - 1] = quantise_s(s_tiles[j - 1])
 
         mask_tiles, g_operands, products = {}, {}, {}
         for j in H_CHUNKS[0]:
             mask_tiles[j] = make_mask(j)
-        for rows in (first_half, second_half):
-            for j in G_BY_SCALAR:
-                if rows == first_half:
-                    g_grouped = g_grouped_pool.tile([P, UNIT_TILES, P, PACK], BF16, align_bytes=64)
-                    g_operands[j] = g_grouped
-                regroup_g(nc.scalar.copy, j, g_operands[j], rows)
-        for j in G_BY_VECTOR:
+        for j in G_BY_SCALAR:
             g_grouped = g_grouped_pool.tile([P, UNIT_TILES, P, PACK], BF16, align_bytes=64)
             g_operands[j] = g_grouped
-            regroup_g(nc.vector.tensor_copy, j, g_grouped, first_half)
+            regroup_g(nc.scalar.copy, j, g_grouped)
 
         def finish(j):
             products[j] = multiply(*quantise_dh(mask_tiles[j]), *s_operands[j])
@@ -226,7 +202,9 @@ def tile_skill_net_pa_v_kernel(tc, s, ei1, ej1, w11, b11, w12, b12, h, grad_out,
             finish(j)
         g_operands[2] = regroup_g_by_tensor(2)
         for j in G_BY_VECTOR:
-            regroup_g(nc.vector.tensor_copy, j, g_operands[j], second_half)
+            g_grouped = g_grouped_pool.tile([P, UNIT_TILES, P, PACK], BF16, align_bytes=64)
+            g_operands[j] = g_grouped
+            regroup_g(nc.vector.tensor_copy, j, g_grouped)
 
         for j in range(2, MODULES):
             mask_tiles[j] = make_mask(j)

@@ -1,5 +1,4 @@
 import concourse.mybir as mybir
-from concourse.masks import make_identity
 
 BF16 = mybir.dt.bfloat16
 F32 = mybir.dt.float32
@@ -19,9 +18,8 @@ UNIT_TILES = UNITS // P
 H_CHUNKS = ((0, 1), (2, 3, 4), (5, 6, 7))
 S_BY_VECTOR = (0, 1, 2, 3)
 S_BY_SCALAR = (4, 5, 6, 7)
-G_BY_TENSOR = (0, 1, 2)
-G_BY_SCALAR = (3, 4, 5)
-G_BY_VECTOR = (6, 7)
+G_BY_SCALAR = (2, 3, 4, 5)
+G_BY_VECTOR = (0, 1, 6, 7)
 SHARED_TAIL = 2
 RESULT_GROUP = 4
 
@@ -37,22 +35,18 @@ def tile_skill_net_pa_v_kernel(tc, s, ei1, ej1, w11, b11, w12, b12, h, grad_out,
     out_rows = out.rearrange("j (m b) f -> j m b f", b=UNIT_TILES)
 
     with (
-        tc.tile_pool(name="constants", bufs=1) as constants,
         tc.tile_pool(name="s_space", bufs=1) as s_space,
         tc.tile_pool(name="g_space", bufs=1) as g_space,
         tc.tile_pool(name="h_loads", bufs=1) as h_loads,
-        tc.tile_pool(name="s_grouped_by_vector", bufs=4) as s_grouped_by_vector,
+        tc.tile_pool(name="s_grouped_by_vector", bufs=2) as s_grouped_by_vector,
         tc.tile_pool(name="s_grouped_by_scalar", bufs=4) as s_grouped_by_scalar,
-        tc.tile_pool(name="g_grouped_pool", bufs=len(G_BY_SCALAR) + len(G_BY_VECTOR)) as g_grouped_pool,
+        tc.tile_pool(name="g_grouped_pool", bufs=6) as g_grouped_pool,
         tc.tile_pool(name="dh_pool", bufs=4) as dh_pool,
         tc.tile_pool(name="s_quantised", bufs=MODULES) as s_quantised,
         tc.tile_pool(name="dh_quantised", bufs=2) as dh_quantised,
         tc.psum_pool(name="psum", bufs=8) as psum,
         tc.manual_schedule(),
     ):
-        identity = constants.tile([P, P], BF16)
-        make_identity(nc, identity[:])
-
         s_in = s_space.tile([P, PACK, MODULES, FEATURES], BF16, name="s_bytes")
         nc.sync.dma_start(out=s_in[:], in_=s_rows)
 
@@ -104,29 +98,8 @@ def tile_skill_net_pa_v_kernel(tc, s, ei1, ej1, w11, b11, w12, b12, h, grad_out,
             )
             return mask
 
-        def regroup_g_by_tensor(j):
-            banks = []
-            loaded_view = g_in[:, :, j, :].rearrange("p t (m b) -> p b m t", b=UNIT_TILES)
-            for first in range(0, UNIT_TILES, 2):
-                acc = psum.tile([P, 2, P, PACK], BF16)
-                for n in range(2):
-                    nc.tensor.matmul(
-                        out=acc[:, n],
-                        lhsT=identity[:],
-                        rhs=loaded_view[:, first + n],
-                        start=True,
-                        stop=True,
-                    )
-                banks.append(acc)
-            return banks
-
         def mask_dh(j, mask):
-            if j in G_BY_TENSOR:
-                for n, bank in enumerate(g_operands[j]):
-                    part = mask[:, 2 * n : 2 * n + 2]
-                    nc.vector.tensor_tensor(out=part, in0=part, in1=bank[:], op=ALU.mult)
-            else:
-                nc.vector.tensor_tensor(out=mask[:], in0=mask[:], in1=g_operands[j][:], op=ALU.mult)
+            nc.vector.tensor_tensor(out=mask[:], in0=mask[:], in1=g_operands[j][:], op=ALU.mult)
 
         def quantise_dh(dh_grouped):
             dh_codes = dh_quantised.tile([P, UNITS], U32, align_bytes=64)
@@ -184,6 +157,13 @@ def tile_skill_net_pa_v_kernel(tc, s, ei1, ej1, w11, b11, w12, b12, h, grad_out,
                 s_operands[j - 1] = quantise_s(s_tiles[j - 1])
 
         mask_tiles, g_operands, products = {}, {}, {}
+        def group_on_vector(j):
+            g_grouped = g_grouped_pool.tile([P, UNIT_TILES, P, PACK], BF16, align_bytes=64)
+            g_operands[j] = g_grouped
+            regroup_g(nc.vector.tensor_copy, j, g_grouped)
+
+        for j in G_BY_VECTOR[:2]:
+            group_on_vector(j)
         for j in H_CHUNKS[0]:
             mask_tiles[j] = make_mask(j)
         for j in G_BY_SCALAR:
@@ -195,16 +175,11 @@ def tile_skill_net_pa_v_kernel(tc, s, ei1, ej1, w11, b11, w12, b12, h, grad_out,
             products[j] = multiply(*quantise_dh(mask_tiles[j]), *s_operands[j])
 
         for j in H_CHUNKS[0]:
-            g_operands[j] = regroup_g_by_tensor(j)
-        for j in H_CHUNKS[0]:
             mask_dh(j, mask_tiles[j])
         for j in H_CHUNKS[0]:
             finish(j)
-        g_operands[2] = regroup_g_by_tensor(2)
-        for j in G_BY_VECTOR:
-            g_grouped = g_grouped_pool.tile([P, UNIT_TILES, P, PACK], BF16, align_bytes=64)
-            g_operands[j] = g_grouped
-            regroup_g(nc.vector.tensor_copy, j, g_grouped)
+        for j in G_BY_VECTOR[2:]:
+            group_on_vector(j)
 
         for j in range(2, MODULES):
             mask_tiles[j] = make_mask(j)

@@ -1,4 +1,5 @@
 import concourse.mybir as mybir
+from concourse.masks import make_identity
 
 BF16 = mybir.dt.bfloat16
 F32 = mybir.dt.float32
@@ -15,12 +16,13 @@ MODULES = 8
 UNITS = 512
 FEATURES = 512
 UNIT_TILES = UNITS // P
-H_CHUNKS = ((0, 1), (2, 3, 4), (5, 6, 7))
-S_BY_VECTOR = (0, 1, 2, 3)
-S_BY_SCALAR = (4, 5, 6, 7)
-G_BY_SCALAR = (2, 3, 4, 5)
-G_BY_VECTOR = (0, 1, 6, 7)
-SHARED_TAIL = 2
+H_CHUNKS = ((0, 1), (2, 3), (4, 5), (6, 7))
+S_BY_VECTOR = (0, 1, 2, 3, 4)
+S_BY_SCALAR = (5, 6, 7)
+G_BY_SCALAR = (0, 3, 4, 5, 6)
+G_BY_TENSOR = (1, 2)
+G_BY_VECTOR = (7,)
+SHARED_TAIL = 1
 RESULT_GROUP = 4
 
 FLOPS = 2 * MODULES * UNITS * FEATURES * ROWS
@@ -35,18 +37,22 @@ def tile_skill_net_pa_v_kernel(tc, s, ei1, ej1, w11, b11, w12, b12, h, grad_out,
     out_rows = out.rearrange("j (m b) f -> j m b f", b=UNIT_TILES)
 
     with (
+        tc.tile_pool(name="constants", bufs=1) as constants,
         tc.tile_pool(name="s_space", bufs=1) as s_space,
         tc.tile_pool(name="g_space", bufs=1) as g_space,
         tc.tile_pool(name="h_loads", bufs=1) as h_loads,
         tc.tile_pool(name="s_grouped_by_vector", bufs=2) as s_grouped_by_vector,
-        tc.tile_pool(name="s_grouped_by_scalar", bufs=4) as s_grouped_by_scalar,
-        tc.tile_pool(name="g_grouped_pool", bufs=6) as g_grouped_pool,
+        tc.tile_pool(name="s_grouped_by_scalar", bufs=len(S_BY_SCALAR)) as s_grouped_by_scalar,
+        tc.tile_pool(name="g_grouped_pool", bufs=len(G_BY_SCALAR) + len(G_BY_VECTOR)) as g_grouped_pool,
         tc.tile_pool(name="dh_pool", bufs=4) as dh_pool,
         tc.tile_pool(name="s_quantised", bufs=MODULES) as s_quantised,
         tc.tile_pool(name="dh_quantised", bufs=2) as dh_quantised,
         tc.psum_pool(name="psum", bufs=8) as psum,
         tc.manual_schedule(),
     ):
+        identity = constants.tile([P, P], BF16)
+        make_identity(nc, identity[:])
+
         s_in = s_space.tile([P, PACK, MODULES, FEATURES], BF16, name="s_bytes")
         nc.sync.dma_start(out=s_in[:], in_=s_rows)
 
@@ -59,10 +65,9 @@ def tile_skill_net_pa_v_kernel(tc, s, ei1, ej1, w11, b11, w12, b12, h, grad_out,
             for n in range(count):
                 h_modules[first + n] = h_in[:, :, n, :]
 
-        load_h(H_CHUNKS[0])
         g_in = g_space.tile([P, PACK, MODULES, UNITS], BF16, name="g_bytes")
         nc.sync.dma_start(out=g_in[:], in_=g_rows)
-        for chunk in H_CHUNKS[1:]:
+        for chunk in H_CHUNKS:
             load_h(chunk)
 
         def regroup_s(copy, j, s_grouped):
@@ -98,8 +103,30 @@ def tile_skill_net_pa_v_kernel(tc, s, ei1, ej1, w11, b11, w12, b12, h, grad_out,
             )
             return mask
 
+        def regroup_g_by_tensor(j):
+            banks = []
+            for k in range(2):
+                units = slice(k * UNITS // 2, (k + 1) * UNITS // 2)
+                acc = psum.tile([P, UNIT_TILES, P // 2, PACK], BF16)
+                for first in range(0, PACK, 2):
+                    rows = slice(first, first + 2)
+                    nc.tensor.matmul(
+                        out=acc[:, :, :, rows].rearrange("p b m t -> p m b t"),
+                        lhsT=identity[:],
+                        rhs=g_in[:, rows, j, units].rearrange("p t (m b) -> p m b t", b=UNIT_TILES),
+                        start=True,
+                        stop=True,
+                    )
+                banks.append(acc)
+            return banks
+
         def mask_dh(j, mask):
-            nc.vector.tensor_tensor(out=mask[:], in0=mask[:], in1=g_operands[j][:], op=ALU.mult)
+            if j in G_BY_TENSOR:
+                for k, bank in enumerate(g_operands[j]):
+                    part = mask[:, :, k * P // 2 : (k + 1) * P // 2, :]
+                    nc.vector.tensor_tensor(out=part, in0=part, in1=bank[:], op=ALU.mult)
+            else:
+                nc.vector.tensor_tensor(out=mask[:], in0=mask[:], in1=g_operands[j][:], op=ALU.mult)
 
         def quantise_dh(dh_grouped):
             dh_codes = dh_quantised.tile([P, UNITS], U32, align_bytes=64)
@@ -157,36 +184,22 @@ def tile_skill_net_pa_v_kernel(tc, s, ei1, ej1, w11, b11, w12, b12, h, grad_out,
                 s_operands[j - 1] = quantise_s(s_tiles[j - 1])
 
         mask_tiles, g_operands, products = {}, {}, {}
-        def group_on_vector(j):
-            g_grouped = g_grouped_pool.tile([P, UNIT_TILES, P, PACK], BF16, align_bytes=64)
-            g_operands[j] = g_grouped
-            regroup_g(nc.vector.tensor_copy, j, g_grouped)
+        for copy, modules in ((nc.scalar.copy, G_BY_SCALAR), (nc.vector.tensor_copy, G_BY_VECTOR)):
+            for j in modules:
+                g_grouped = g_grouped_pool.tile([P, UNIT_TILES, P, PACK], BF16, align_bytes=64)
+                g_operands[j] = g_grouped
+                regroup_g(copy, j, g_grouped)
+        for j in G_BY_TENSOR:
+            g_operands[j] = regroup_g_by_tensor(j)
 
-        for j in G_BY_VECTOR[:2]:
-            group_on_vector(j)
-        for j in H_CHUNKS[0]:
-            mask_tiles[j] = make_mask(j)
-        for j in G_BY_SCALAR:
-            g_grouped = g_grouped_pool.tile([P, UNIT_TILES, P, PACK], BF16, align_bytes=64)
-            g_operands[j] = g_grouped
-            regroup_g(nc.scalar.copy, j, g_grouped)
-
-        def finish(j):
-            products[j] = multiply(*quantise_dh(mask_tiles[j]), *s_operands[j])
-
-        for j in H_CHUNKS[0]:
-            mask_dh(j, mask_tiles[j])
-        for j in H_CHUNKS[0]:
-            finish(j)
-        for j in G_BY_VECTOR[2:]:
-            group_on_vector(j)
-
-        for j in range(2, MODULES):
-            mask_tiles[j] = make_mask(j)
-            if j > 2:
-                finish(j - 1)
-            mask_dh(j, mask_tiles[j])
-            store(j - 2, products[j - 2])
-        finish(MODULES - 1)
-        for j in range(MODULES - SHARED_TAIL, MODULES):
+        for j in range(MODULES + 1):
+            if j < MODULES:
+                mask_tiles[j] = make_mask(j)
+            if j >= 1:
+                products[j - 1] = multiply(*quantise_dh(mask_tiles[j - 1]), *s_operands[j - 1])
+            if j < MODULES:
+                mask_dh(j, mask_tiles[j])
+            if 2 <= j <= MODULES - 1:
+                store(j - 2, products[j - 2])
+        for j in (MODULES - 2, MODULES - 1):
             store(j, products[j])

import concourse.mybir as mybir
from concourse.masks import make_identity

BF16 = mybir.dt.bfloat16
F32 = mybir.dt.float32
U32 = mybir.dt.uint32
U8 = mybir.dt.uint8
E4M3_X4 = mybir.dt.float8_e4m3fn_x4
E5M2_X4 = mybir.dt.float8_e5m2_x4
ALU = mybir.AluOpType

P = 128
PACK = 4
ROWS = P * PACK
MODULES = 8
UNITS = 512
FEATURES = 512
UNIT_TILES = UNITS // P
H_CHUNKS = ((0, 1), (2, 3), (4, 5), (6, 7))
S_BY_VECTOR = (0, 1, 2, 3, 4)
S_BY_SCALAR = (5, 6, 7)
G_BY_SCALAR = (0, 3, 4, 5, 6)
G_BY_TENSOR = (1, 2)
G_BY_VECTOR = (7,)
SHARED_TAIL = 1
RESULT_GROUP = 4

FLOPS = 2 * MODULES * UNITS * FEATURES * ROWS
BYTES = MODULES * ROWS * (2 * FEATURES + 2 * UNITS + 4 * UNITS) + 4 * MODULES * UNITS * FEATURES

def tile_skill_net_pa_v_kernel(tc, s, ei1, ej1, w11, b11, w12, b12, h, grad_out, out):
    nc = tc.nc

    s_rows = s.rearrange("(p t) j f -> p t j f", t=PACK)
    g_rows = grad_out.rearrange("(p t) j l -> p t j l", t=PACK)
    h_rows = h.rearrange("(p t) j l -> p t j l", t=PACK)
    out_rows = out.rearrange("j (m b) f -> j m b f", b=UNIT_TILES)

    with (
        tc.tile_pool(name="constants", bufs=1) as constants,
        tc.tile_pool(name="s_space", bufs=1) as s_space,
        tc.tile_pool(name="g_space", bufs=1) as g_space,
        tc.tile_pool(name="h_loads", bufs=1) as h_loads,
        tc.tile_pool(name="s_grouped_by_vector", bufs=2) as s_grouped_by_vector,
        tc.tile_pool(name="s_grouped_by_scalar", bufs=len(S_BY_SCALAR)) as s_grouped_by_scalar,
        tc.tile_pool(name="g_grouped_pool", bufs=len(G_BY_SCALAR) + len(G_BY_VECTOR)) as g_grouped_pool,
        tc.tile_pool(name="dh_pool", bufs=4) as dh_pool,
        tc.tile_pool(name="s_quantised", bufs=MODULES) as s_quantised,
        tc.tile_pool(name="dh_quantised", bufs=2) as dh_quantised,
        tc.psum_pool(name="psum", bufs=8) as psum,
        tc.manual_schedule(),
    ):
        identity = constants.tile([P, P], BF16)
        make_identity(nc, identity[:])

        s_in = s_space.tile([P, PACK, MODULES, FEATURES], BF16, name="s_bytes")
        nc.sync.dma_start(out=s_in[:], in_=s_rows)

        h_modules = {}

        def load_h(chunk):
            first, count = chunk[0], len(chunk)
            h_in = h_loads.tile([P, PACK, count, UNITS], F32, name="h_in_%d" % first)
            nc.sync.dma_start(out=h_in[:], in_=h_rows[:, :, first : first + count, :])
            for n in range(count):
                h_modules[first + n] = h_in[:, :, n, :]

        g_in = g_space.tile([P, PACK, MODULES, UNITS], BF16, name="g_bytes")
        nc.sync.dma_start(out=g_in[:], in_=g_rows)
        for chunk in H_CHUNKS:
            load_h(chunk)

        def regroup_s(copy, j, s_grouped):
            copy(
                out=s_grouped[:].rearrange("p (c i) t -> p c t i", i=4),
                in_=s_in[:, :, j, :].rearrange("p t (c i) -> p c t i", i=4),
            )

        def regroup_g(copy, j, g_grouped):
            copy(
                out=g_grouped[:].rearrange("p b m t -> p m t b"),
                in_=g_in[:, :, j, :].rearrange("p t (m b) -> p m t b", b=UNIT_TILES),
            )

        def quantise_s(s_grouped):
            s_codes = s_quantised.tile([P, FEATURES], U32, align_bytes=64)
            s_scales = s_quantised.tile([P, FEATURES], U8, align_bytes=64)
            nc.vector.quantize_mx(
                out=s_codes[:].bitcast(E4M3_X4),
                scales=s_scales[:],
                in_=s_grouped[:].rearrange("p f t -> p (f t)"),
            )
            return s_codes, s_scales

        def make_mask(j):
            mask = dh_pool.tile([P, UNIT_TILES, P, PACK], BF16, align_bytes=64)
            nc.vector.tensor_scalar(
                out=mask[:].rearrange("p b m t -> p m t b"),
                in0=h_modules[j].rearrange("p t (m b) -> p m t b", b=UNIT_TILES),
                scalar1=0.0,
                scalar2=None,
                op0=ALU.is_gt,
            )
            return mask

        def regroup_g_by_tensor(j):
            banks = []
            for k in range(2):
                units = slice(k * UNITS // 2, (k + 1) * UNITS // 2)
                acc = psum.tile([P, UNIT_TILES, P // 2, PACK], BF16)
                for first in range(0, PACK, 2):
                    rows = slice(first, first + 2)
                    nc.tensor.matmul(
                        out=acc[:, :, :, rows].rearrange("p b m t -> p m b t"),
                        lhsT=identity[:],
                        rhs=g_in[:, rows, j, units].rearrange("p t (m b) -> p m b t", b=UNIT_TILES),
                        start=True,
                        stop=True,
                    )
                banks.append(acc)
            return banks

        def mask_dh(j, mask):
            if j in G_BY_TENSOR:
                for k, bank in enumerate(g_operands[j]):
                    part = mask[:, :, k * P // 2 : (k + 1) * P // 2, :]
                    nc.vector.tensor_tensor(out=part, in0=part, in1=bank[:], op=ALU.mult)
            else:
                nc.vector.tensor_tensor(out=mask[:], in0=mask[:], in1=g_operands[j][:], op=ALU.mult)

        def quantise_dh(dh_grouped):
            dh_codes = dh_quantised.tile([P, UNITS], U32, align_bytes=64)
            dh_scales = dh_quantised.tile([P, UNITS], U8, align_bytes=64)
            nc.vector.quantize_mx(
                out=dh_codes[:].bitcast(E5M2_X4),
                scales=dh_scales[:],
                in_=dh_grouped[:].rearrange("p b m t -> p (b m t)"),
            )
            return dh_codes, dh_scales

        def multiply(dh_codes, dh_scales, s_codes, s_scales):
            banks = []
            for b in range(UNIT_TILES):
                units = slice(b * P, (b + 1) * P)
                acc = psum.tile([P, FEATURES], F32)
                nc.tensor.matmul_mx(
                    out=acc[:],
                    lhsT=dh_codes[:, units].bitcast(E5M2_X4),
                    lhsT_scale=dh_scales[:, units],
                    rhs=s_codes[:].bitcast(E4M3_X4),
                    rhs_scale=s_scales[:],
                    start=True,
                    stop=True,
                )
                banks.append(acc)
            return banks

        result_groups = {}

        def store(j, banks):
            group, place = divmod(j, RESULT_GROUP)
            if place == 0:
                space, name = (s_space, "s_bytes") if group == 0 else (g_space, "g_bytes")
                result_groups[group] = space.tile([P, RESULT_GROUP, UNIT_TILES, FEATURES], F32, name=name)
            result = result_groups[group][:, place]
            for b in range(UNIT_TILES):
                if j >= MODULES - SHARED_TAIL and b % 2 == 1:
                    nc.vector.tensor_copy(out=result[:, b, :], in_=banks[b][:])
                else:
                    nc.scalar.copy(out=result[:, b, :], in_=banks[b][:])
            nc.sync.dma_start(out=out_rows[j], in_=result)

        s_tiles, s_operands = {}, {}
        for j in S_BY_SCALAR:
            s_grouped = s_grouped_by_scalar.tile([P, FEATURES, PACK], BF16, align_bytes=64)
            s_tiles[j] = s_grouped
            regroup_s(nc.scalar.copy, j, s_grouped)
        for j in range(MODULES + 1):
            if j in S_BY_VECTOR:
                s_grouped = s_grouped_by_vector.tile([P, FEATURES, PACK], BF16, align_bytes=64)
                s_tiles[j] = s_grouped
                regroup_s(nc.vector.tensor_copy, j, s_grouped)
            if j >= 1:
                s_operands[j - 1] = quantise_s(s_tiles[j - 1])

        mask_tiles, g_operands, products = {}, {}, {}
        for copy, modules in ((nc.scalar.copy, G_BY_SCALAR), (nc.vector.tensor_copy, G_BY_VECTOR)):
            for j in modules:
                g_grouped = g_grouped_pool.tile([P, UNIT_TILES, P, PACK], BF16, align_bytes=64)
                g_operands[j] = g_grouped
                regroup_g(copy, j, g_grouped)
        for j in G_BY_TENSOR:
            g_operands[j] = regroup_g_by_tensor(j)

        for j in range(MODULES + 1):
            if j < MODULES:
                mask_tiles[j] = make_mask(j)
            if j >= 1:
                products[j - 1] = multiply(*quantise_dh(mask_tiles[j - 1]), *s_operands[j - 1])
            if j < MODULES:
                mask_dh(j, mask_tiles[j])
            if 2 <= j <= MODULES - 1:
                store(j - 2, products[j - 2])
        for j in (MODULES - 2, MODULES - 1):
            store(j, products[j])
